import numpy as np
import ml_dtypes


def mxq(x, axis, fmt="e4m3"):
    dtype, down = {"e4m3": (ml_dtypes.float8_e4m3fn, 7), "e5m2": (ml_dtypes.float8_e5m2, 14)}[fmt]
    v = np.moveaxis(np.asarray(x, np.float32).astype(ml_dtypes.bfloat16).astype(np.float64), axis, -1)
    blocks = v.reshape(v.shape[:-1] + (-1, 32))
    amax = np.abs(blocks).max(-1, keepdims=True)
    byte = np.maximum(np.where(amax > 0, np.frexp(amax)[1] - 1 + 127, 0) - down, 1)
    scale = np.exp2(byte - 127.0)
    codes = (blocks / scale).astype(np.float32).astype(dtype).astype(np.float64)
    return np.moveaxis((codes * scale).reshape(v.shape), -1, axis)


WIDE = False


def mx_kscale(k):
    if not WIDE:
        return np.ones(k)
    levels = np.array([10, -10, 5, -5, 0])
    a = np.random.permutation(np.resize(levels, k // 512 * 4)).reshape(k // 512, 4)
    idx = np.arange(k)
    return np.exp2(a[idx // 512, idx % 128 // 32])


BF16 = ml_dtypes.bfloat16


def bf(x):
    return np.asarray(x, np.float32).astype(BF16)


def f64(x):
    return np.asarray(x).astype(np.float64)


B, S, H, R = 4, 1024, 1024, 512
G = H // R


def setup_inputs():
    s = mx_kscale(R)
    return {"x": bf(np.random.standard_normal((B, S, H)) * np.tile(s, G)),
            "matrix": bf(np.random.standard_normal((R, R)) / np.sqrt(R) / s[:, None])}


def reference(x, matrix):
    x, matrix = f64(x), f64(matrix)
    b, n, h = x.shape
    r = matrix.shape[0]
    g = h // r
    compressed = x.reshape(b, n, g, r).sum(axis=2)
    out = mxq(compressed, 2, "e4m3") @ mxq(matrix, 0, "e4m3")
    return np.repeat(out, g, axis=2)[:, :, :h]

@@ -1,0 +1,125 @@
+from contextlib import ExitStack
+
+import concourse.mybir as mybir
+from concourse.masks import make_identity
+
+BF16 = mybir.dt.bfloat16
+F32 = mybir.dt.float32
+U32 = mybir.dt.uint32
+U8 = mybir.dt.uint8
+FP8X4 = mybir.dt.float8_e4m3fn_x4
+
+P = 128
+PACK = 4
+TOKENS = 4096
+H = 1024
+R = 512
+N_TILES = TOKENS // P
+PAIRS = N_TILES // 2
+LOAD_TILES = (2, 2, 4, 8, 8, 8)
+STORE_TILES = 4
+
+FLOPS = 2 * TOKENS * R * R
+
+
+def tile_mora_t_kernel(tc, x, matrix, out):
+    nc = tc.nc
+    x_rows = x.flatten_outer_dims().rearrange("(p i) h -> p i h", i=N_TILES)
+    out_rows = out.flatten_outer_dims().rearrange("(p i) h -> p i h", i=N_TILES)
+
+    with ExitStack() as ctx:
+        keep = ctx.enter_context(tc.tile_pool(name="keep", bufs=1))
+        work = ctx.enter_context(tc.tile_pool(name="work", bufs=3))
+        stage = ctx.enter_context(tc.tile_pool(name="stage", bufs=N_TILES // STORE_TILES))
+        flip = ctx.enter_context(tc.psum_pool(name="flip", bufs=3))
+        sums = ctx.enter_context(tc.psum_pool(name="sums", bufs=5))
+        ctx.enter_context(tc.manual_schedule())
+
+        ident = keep.tile([P, P], BF16, name="ident")
+        make_identity(nc, ident[:])
+
+        where = {}
+        w_raw = keep.tile([P, PACK, R], BF16, name="w_raw")
+        first = 0
+        for n, width in enumerate(LOAD_TILES):
+            x_sb = keep.tile([P, width, H], BF16, name="x_sb%d" % n)
+            nc.sync.dma_start(out=x_sb[:], in_=x_rows[:, first : first + width, :])
+            for j in range(0, width, 2):
+                where[(first + j) // 2] = (x_sb, j)
+            first += width
+            if n == 0:
+                nc.sync.dma_start(out=w_raw[:], in_=matrix.rearrange("(t p) n -> p t n", p=P))
+
+        w_grouped = keep.tile([P, R, PACK], BF16, name="w_grouped", align_bytes=64)
+        w_codes = keep.tile([P, R], U32, name="w_codes", align_bytes=64)
+        w_scales = keep.tile([P, R], U8, name="w_scales", align_bytes=64)
+        nc.scalar.copy(out=w_grouped[:], in_=w_raw[:].rearrange("p t n -> p n t"))
+
+        c_of = {}
+        flipped_of = {}
+        grouped_of = {}
+        staged_of = {}
+
+        def add_and_transpose(g):
+            x_sb, j = where[g]
+            c = work.tile([P, 2, R], BF16, name="c", tag="c")
+            nc.vector.tensor_tensor(
+                out=c[:], in0=x_sb[:, j : j + 2, 0:R], in1=x_sb[:, j : j + 2, R:H], op=mybir.AluOpType.add
+            )
+            flipped = flip.tile([P, 2, PACK, P], BF16, name="flipped", tag="flipped")
+            for i in range(2):
+                for t in range(PACK):
+                    nc.tensor.transpose(flipped[:, i, t, :], c[:, i, t * P : (t + 1) * P], ident[:])
+            flipped_of[g] = flipped
+
+        def regroup(g):
+            grouped = work.tile([P, 2, P, PACK], BF16, name="grouped", tag="grouped", align_bytes=64)
+            nc.vector.tensor_copy(out=grouped[:], in_=flipped_of[g][:].rearrange("p i t r -> p i r t"))
+            grouped_of[g] = grouped
+
+        def multiply(g):
+            codes = work.tile([P, 2 * P], U32, name="codes", tag="codes", align_bytes=64)
+            scales = work.tile([P, 2 * P], U8, name="scales", tag="scales", align_bytes=64)
+            nc.vector.quantize_mx(
+                out=codes[:].bitcast(FP8X4),
+                scales=scales[:],
+                in_=grouped_of[g][:].rearrange("p i r t -> p (i r t)"),
+            )
+            s = (2 * g) // STORE_TILES
+            if (2 * g) % STORE_TILES == 0:
+                staged = stage.tile([P, STORE_TILES, H], F32, name="staged", tag="staged")
+                staged_of[s] = staged
+            staged = staged_of[s]
+            for i in range(2):
+                acc = sums.tile([P, R], F32, name="acc", tag="acc")
+                nc.tensor.matmul_mx(
+                    out=acc[:],
+                    lhsT=codes[:, i * P : (i + 1) * P].bitcast(FP8X4),
+                    lhsT_scale=scales[:, i * P : (i + 1) * P],
+                    rhs=w_codes[:].bitcast(FP8X4),
+                    rhs_scale=w_scales[:],
+                    start=True,
+                    stop=True,
+                )
+                nc.scalar.copy(
+                    out=staged[:, (2 * g + i) % STORE_TILES, :].rearrange("p (k r) -> p k r", r=2),
+                    in_=acc[:].unsqueeze(2).to_broadcast([P, R, 2]),
+                )
+            if (2 * g + 2) % STORE_TILES == 0:
+                nc.sync.dma_start(
+                    out=out_rows[:, s * STORE_TILES : (s + 1) * STORE_TILES, :], in_=staged[:]
+                )
+
+        for step in range(PAIRS + 2):
+            if step < PAIRS:
+                add_and_transpose(step)
+            if 0 <= step - 1 < PAIRS:
+                regroup(step - 1)
+            if step == 1:
+                nc.vector.quantize_mx(
+                    out=w_codes[:].bitcast(FP8X4),
+                    scales=w_scales[:],
+                    in_=w_grouped[:].rearrange("p n t -> p (n t)"),
+                )
+            if 0 <= step - 2 < PAIRS:
+                multiply(step - 2)

@@ -17,7 +17,8 @@ R = 512
 N_TILES = TOKENS // P
 PAIRS = N_TILES // 2
 LOAD_TILES = (2, 2, 4, 8, 8, 8)
-STORE_TILES = 4
+STORE_TILES = (4, 4, 4, 4, 4, 4, 4, 2, 2)
+VECTOR_DRAINS = (11, 21, 31)
 
 FLOPS = 2 * TOKENS * R * R
 
@@ -30,7 +31,6 @@ def tile_mora_t_kernel(tc, x, matrix, out):
     with ExitStack() as ctx:
         keep = ctx.enter_context(tc.tile_pool(name="keep", bufs=1))
         work = ctx.enter_context(tc.tile_pool(name="work", bufs=3))
-        stage = ctx.enter_context(tc.tile_pool(name="stage", bufs=N_TILES // STORE_TILES))
         flip = ctx.enter_context(tc.psum_pool(name="flip", bufs=3))
         sums = ctx.enter_context(tc.psum_pool(name="sums", bufs=5))
         ctx.enter_context(tc.manual_schedule())
@@ -55,10 +55,17 @@ def tile_mora_t_kernel(tc, x, matrix, out):
         w_scales = keep.tile([P, R], U8, name="w_scales", align_bytes=64)
         nc.scalar.copy(out=w_grouped[:], in_=w_raw[:].rearrange("p t n -> p n t"))
 
-        c_of = {}
+        staged_of = {}
+        first = 0
+        for n, width in enumerate(STORE_TILES):
+            staged = keep.tile([P, width, H], F32, name="staged%d" % n)
+            for j in range(width):
+                staged_of[first + j] = (staged, j, first, width)
+            first += width
+        left = {}
+
         flipped_of = {}
         grouped_of = {}
-        staged_of = {}
 
         def add_and_transpose(g):
             x_sb, j = where[g]
@@ -77,6 +84,18 @@ def tile_mora_t_kernel(tc, x, matrix, out):
             nc.vector.tensor_copy(out=grouped[:], in_=flipped_of[g][:].rearrange("p i t r -> p i r t"))
             grouped_of[g] = grouped
 
+        def drain(tile_index, acc):
+            staged, j, start, width = staged_of[tile_index]
+            dst = staged[:, j, :].rearrange("p (k r) -> p k r", r=2)
+            src = acc[:].unsqueeze(2).to_broadcast([P, R, 2])
+            if tile_index in VECTOR_DRAINS:
+                nc.vector.tensor_copy(out=dst, in_=src)
+            else:
+                nc.scalar.copy(out=dst, in_=src)
+            left[start] = left.get(start, width) - 1
+            if left[start] == 0:
+                nc.sync.dma_start(out=out_rows[:, start : start + width, :], in_=staged[:])
+
         def multiply(g):
             codes = work.tile([P, 2 * P], U32, name="codes", tag="codes", align_bytes=64)
             scales = work.tile([P, 2 * P], U8, name="scales", tag="scales", align_bytes=64)
@@ -85,11 +104,7 @@ def tile_mora_t_kernel(tc, x, matrix, out):
                 scales=scales[:],
                 in_=grouped_of[g][:].rearrange("p i r t -> p (i r t)"),
             )
-            s = (2 * g) // STORE_TILES
-            if (2 * g) % STORE_TILES == 0:
-                staged = stage.tile([P, STORE_TILES, H], F32, name="staged", tag="staged")
-                staged_of[s] = staged
-            staged = staged_of[s]
+            later = []
             for i in range(2):
                 acc = sums.tile([P, R], F32, name="acc", tag="acc")
                 nc.tensor.matmul_mx(
@@ -101,25 +116,28 @@ def tile_mora_t_kernel(tc, x, matrix, out):
                     start=True,
                     stop=True,
                 )
-                nc.scalar.copy(
-                    out=staged[:, (2 * g + i) % STORE_TILES, :].rearrange("p (k r) -> p k r", r=2),
-                    in_=acc[:].unsqueeze(2).to_broadcast([P, R, 2]),
-                )
-            if (2 * g + 2) % STORE_TILES == 0:
-                nc.sync.dma_start(
-                    out=out_rows[:, s * STORE_TILES : (s + 1) * STORE_TILES, :], in_=staged[:]
-                )
+                if 2 * g + i in VECTOR_DRAINS:
+                    later.append((2 * g + i, acc))
+                else:
+                    drain(2 * g + i, acc)
+            return later
 
-        for step in range(PAIRS + 2):
-            if step < PAIRS:
-                add_and_transpose(step)
-            if 0 <= step - 1 < PAIRS:
-                regroup(step - 1)
-            if step == 1:
+        add_and_transpose(0)
+        add_and_transpose(1)
+        waiting = []
+        for g in range(PAIRS):
+            regroup(g)
+            if g == 0:
                 nc.vector.quantize_mx(
                     out=w_codes[:].bitcast(FP8X4),
                     scales=w_scales[:],
                     in_=w_grouped[:].rearrange("p n t -> p (n t)"),
                 )
-            if 0 <= step - 2 < PAIRS:
-                multiply(step - 2)
+            if g + 2 < PAIRS:
+                add_and_transpose(g + 2)
+            later = multiply(g)
+            for tile_index, acc in waiting:
+                drain(tile_index, acc)
+            waiting = later
+        for tile_index, acc in waiting:
+            drain(tile_index, acc)

@@ -16,8 +16,8 @@ H = 1024
 R = 512
 N_TILES = TOKENS // P
 PAIRS = N_TILES // 2
-LOAD_TILES = (2, 2, 4, 8, 8, 8)
-STORE_TILES = (4, 4, 4, 4, 4, 4, 4, 2, 2)
+LOAD_TILES = (2, 2, 4, 8, 16)
+STORE_TILES = (8, 8, 8, 4, 4)
 VECTOR_DRAINS = (11, 21, 31)
 
 FLOPS = 2 * TOKENS * R * R
@@ -48,7 +48,10 @@ def tile_mora_t_kernel(tc, x, matrix, out):
                 where[(first + j) // 2] = (x_sb, j)
             first += width
             if n == 0:
-                nc.sync.dma_start(out=w_raw[:], in_=matrix.rearrange("(t p) n -> p t n", p=P))
+                nc.sync.dma_start(
+                    out=w_raw[:].rearrange("p (u e) n -> p u (e n)", e=2),
+                    in_=matrix.rearrange("(u p e) n -> p u (e n)", u=2, e=2),
+                )
 
         w_grouped = keep.tile([P, R, PACK], BF16, name="w_grouped", align_bytes=64)
         w_codes = keep.tile([P, R], U32, name="w_codes", align_bytes=64)
@@ -75,8 +78,9 @@ def tile_mora_t_kernel(tc, x, matrix, out):
             )
             flipped = flip.tile([P, 2, PACK, P], BF16, name="flipped", tag="flipped")
             for i in range(2):
+                planes = c[:, i, :].rearrange("p (u q e) -> p u e q", u=2, e=2)
                 for t in range(PACK):
-                    nc.tensor.transpose(flipped[:, i, t, :], c[:, i, t * P : (t + 1) * P], ident[:])
+                    nc.tensor.transpose(flipped[:, i, t, :], planes[:, t // 2, t % 2, :], ident[:])
             flipped_of[g] = flipped
 
         def regroup(g):

@@ -17,7 +17,7 @@ R = 512
 N_TILES = TOKENS // P
 PAIRS = N_TILES // 2
 LOAD_TILES = (2, 2, 4, 8, 16)
-STORE_TILES = (8, 8, 8, 4, 4)
+STORE_TILES = (4, 6, 6, 6, 6, 4)
 VECTOR_DRAINS = (11, 21, 31)
 
 FLOPS = 2 * TOKENS * R * R

from contextlib import ExitStack

import concourse.mybir as mybir
from concourse.masks import make_identity

BF16 = mybir.dt.bfloat16
F32 = mybir.dt.float32
U32 = mybir.dt.uint32
U8 = mybir.dt.uint8
FP8X4 = mybir.dt.float8_e4m3fn_x4

P = 128
PACK = 4
TOKENS = 4096
H = 1024
R = 512
N_TILES = TOKENS // P
PAIRS = N_TILES // 2
LOAD_TILES = (2, 2, 4, 8, 16)
STORE_TILES = (4, 6, 6, 6, 6, 4)
VECTOR_DRAINS = (11, 21, 31)

FLOPS = 2 * TOKENS * R * R


def tile_mora_t_kernel(tc, x, matrix, out):
    nc = tc.nc
    x_rows = x.flatten_outer_dims().rearrange("(p i) h -> p i h", i=N_TILES)
    out_rows = out.flatten_outer_dims().rearrange("(p i) h -> p i h", i=N_TILES)

    with ExitStack() as ctx:
        keep = ctx.enter_context(tc.tile_pool(name="keep", bufs=1))
        work = ctx.enter_context(tc.tile_pool(name="work", bufs=3))
        flip = ctx.enter_context(tc.psum_pool(name="flip", bufs=3))
        sums = ctx.enter_context(tc.psum_pool(name="sums", bufs=5))
        ctx.enter_context(tc.manual_schedule())

        ident = keep.tile([P, P], BF16, name="ident")
        make_identity(nc, ident[:])

        where = {}
        w_raw = keep.tile([P, PACK, R], BF16, name="w_raw")
        first = 0
        for n, width in enumerate(LOAD_TILES):
            x_sb = keep.tile([P, width, H], BF16, name="x_sb%d" % n)
            nc.sync.dma_start(out=x_sb[:], in_=x_rows[:, first : first + width, :])
            for j in range(0, width, 2):
                where[(first + j) // 2] = (x_sb, j)
            first += width
            if n == 0:
                nc.sync.dma_start(
                    out=w_raw[:].rearrange("p (u e) n -> p u (e n)", e=2),
                    in_=matrix.rearrange("(u p e) n -> p u (e n)", u=2, e=2),
                )

        w_grouped = keep.tile([P, R, PACK], BF16, name="w_grouped", align_bytes=64)
        w_codes = keep.tile([P, R], U32, name="w_codes", align_bytes=64)
        w_scales = keep.tile([P, R], U8, name="w_scales", align_bytes=64)
        nc.scalar.copy(out=w_grouped[:], in_=w_raw[:].rearrange("p t n -> p n t"))

        staged_of = {}
        first = 0
        for n, width in enumerate(STORE_TILES):
            staged = keep.tile([P, width, H], F32, name="staged%d" % n)
            for j in range(width):
                staged_of[first + j] = (staged, j, first, width)
            first += width
        left = {}

        flipped_of = {}
        grouped_of = {}

        def add_and_transpose(g):
            x_sb, j = where[g]
            c = work.tile([P, 2, R], BF16, name="c", tag="c")
            nc.vector.tensor_tensor(
                out=c[:], in0=x_sb[:, j : j + 2, 0:R], in1=x_sb[:, j : j + 2, R:H], op=mybir.AluOpType.add
            )
            flipped = flip.tile([P, 2, PACK, P], BF16, name="flipped", tag="flipped")
            for i in range(2):
                planes = c[:, i, :].rearrange("p (u q e) -> p u e q", u=2, e=2)
                for t in range(PACK):
                    nc.tensor.transpose(flipped[:, i, t, :], planes[:, t // 2, t % 2, :], ident[:])
            flipped_of[g] = flipped

        def regroup(g):
            grouped = work.tile([P, 2, P, PACK], BF16, name="grouped", tag="grouped", align_bytes=64)
            nc.vector.tensor_copy(out=grouped[:], in_=flipped_of[g][:].rearrange("p i t r -> p i r t"))
            grouped_of[g] = grouped

        def drain(tile_index, acc):
            staged, j, start, width = staged_of[tile_index]
            dst = staged[:, j, :].rearrange("p (k r) -> p k r", r=2)
            src = acc[:].unsqueeze(2).to_broadcast([P, R, 2])
            if tile_index in VECTOR_DRAINS:
                nc.vector.tensor_copy(out=dst, in_=src)
            else:
                nc.scalar.copy(out=dst, in_=src)
            left[start] = left.get(start, width) - 1
            if left[start] == 0:
                nc.sync.dma_start(out=out_rows[:, start : start + width, :], in_=staged[:])

        def multiply(g):
            codes = work.tile([P, 2 * P], U32, name="codes", tag="codes", align_bytes=64)
            scales = work.tile([P, 2 * P], U8, name="scales", tag="scales", align_bytes=64)
            nc.vector.quantize_mx(
                out=codes[:].bitcast(FP8X4),
                scales=scales[:],
                in_=grouped_of[g][:].rearrange("p i r t -> p (i r t)"),
            )
            later = []
            for i in range(2):
                acc = sums.tile([P, R], F32, name="acc", tag="acc")
                nc.tensor.matmul_mx(
                    out=acc[:],
                    lhsT=codes[:, i * P : (i + 1) * P].bitcast(FP8X4),
                    lhsT_scale=scales[:, i * P : (i + 1) * P],
                    rhs=w_codes[:].bitcast(FP8X4),
                    rhs_scale=w_scales[:],
                    start=True,
                    stop=True,
                )
                if 2 * g + i in VECTOR_DRAINS:
                    later.append((2 * g + i, acc))
                else:
                    drain(2 * g + i, acc)
            return later

        add_and_transpose(0)
        add_and_transpose(1)
        waiting = []
        for g in range(PAIRS):
            regroup(g)
            if g == 0:
                nc.vector.quantize_mx(
                    out=w_codes[:].bitcast(FP8X4),
                    scales=w_scales[:],
                    in_=w_grouped[:].rearrange("p n t -> p (n t)"),
                )
            if g + 2 < PAIRS:
                add_and_transpose(g + 2)
            later = multiply(g)
            for tile_index, acc in waiting:
                drain(tile_index, acc)
            waiting = later
        for tile_index, acc in waiting:
            drain(tile_index, acc)
